import numpy as np
import ml_dtypes


BF16 = ml_dtypes.bfloat16


def bf(x):
    return np.asarray(x, np.float32).astype(BF16)


def f64(x):
    return np.asarray(x).astype(np.float64)


E2M1 = np.array([0.0, 0.5, 1.0, 1.5, 2.0, 3.0, 4.0, 6.0, -0.0, -0.5, -1.0, -1.5, -2.0, -3.0, -4.0, -6.0])


def pack_weight(w, fmt):
    k, n = w.shape
    w = f64(bf(w)).reshape(k // 32, 32, n)
    amax = np.abs(w).max(1)
    if fmt == "e4m3":
        byte = np.frexp(amax)[1] - 1 + 127 - 7
    else:
        mant, ex = np.frexp(amax / 6.0)
        byte = np.where(mant > 0.5, ex, ex - 1) + 127
    byte = np.clip(np.where(amax > 0, byte, 1), 1, 254)
    scaled = (w * np.exp2(127.0 - byte)[:, None, :]).reshape(k, n).astype(np.float32)
    by_word = np.ascontiguousarray(scaled.reshape(k // 512, 128, 4, n).transpose(0, 1, 3, 2))
    if fmt == "e4m3":
        words = by_word.astype(ml_dtypes.float8_e4m3fn).view(np.uint8)
    else:
        c = by_word.astype(ml_dtypes.float4_e2m1fn).view(np.uint8) & 0xF
        words = c[..., 0::2] | (c[..., 1::2] << 4)
    return np.ascontiguousarray(words), np.ascontiguousarray(byte.astype(np.uint8).reshape(k // 512, 16, n))


def unpack_weight(words, scales, fmt):
    g, p, n, _ = words.shape
    if fmt == "e4m3":
        vals = np.ascontiguousarray(words).view(ml_dtypes.float8_e4m3fn).astype(np.float64)
    else:
        nib = np.empty((g, p, n, 4), np.uint8)
        nib[..., 0::2] = words & 0xF
        nib[..., 1::2] = words >> 4
        vals = E2M1[nib]
    vals = vals * np.repeat(np.exp2(scales.astype(np.float64) - 127.0), 8, axis=1)[..., None]
    return vals.transpose(0, 1, 3, 2).reshape(g * 512, n)

def pack4(w):
    words, scales = pack_weight(w, "e2m1")
    return words.reshape(words.shape[0], 128, -1), scales


def unpack4(words, scales):
    return unpack_weight(words.reshape(words.shape[0], 128, -1, 2), scales, "e2m1")


def kspread(k):
    return np.exp2(np.repeat(np.random.randint(-6, 7, k // 32), 32).astype(np.float64))


B, H, L, DM, DK, DV = 2, 2, 512, 4096, 1024, 2048


def rotate_every_two(x):
    x1 = x[..., ::2]
    x2 = x[..., 1::2]
    return np.stack((-x2, x1), axis=-1).reshape(x.shape)


def xpos_sincos(length, dim):
    angle = 1.0 / (10000.0 ** np.linspace(0.0, 1.0, dim // 2))
    angle = np.repeat(angle, 2)
    idx = f64(np.arange(length))
    angles = idx[:, None] * angle[None, :]
    return np.sin(angles), np.cos(angles)


def setup_inputs():
    s = kspread(DM)
    X = np.random.standard_normal((B, H, L, DM)) * s
    X_words, X_scales = pack4(np.ascontiguousarray(X.reshape(B * H * L, DM).T))
    q_words, q_scales = pack4(np.random.standard_normal((DM, DK)) * 3.0 / np.sqrt(DM) / s[:, None])
    k_words, k_scales = pack4(np.random.standard_normal((DM, DK)) * 3.0 / np.sqrt(DM) / s[:, None])
    return {"X_words": X_words, "X_scales": X_scales,
            "W_Q_words": q_words, "W_Q_scales": q_scales,
            "W_K_words": k_words, "W_K_scales": k_scales}


def reference(X_words, X_scales, W_Q_words, W_Q_scales, W_K_words, W_K_scales):
    xq = unpack4(X_words, X_scales).T.reshape(B, H, L, DM)
    q = xq @ unpack4(W_Q_words, W_Q_scales)
    k = xq @ unpack4(W_K_words, W_K_scales)
    sin, cos = xpos_sincos(L, DK)
    q_rot = q * cos + rotate_every_two(q) * sin
    k_rot = k * cos + rotate_every_two(k) * (-sin)
    return (q_rot, k_rot)

@@ -1,0 +1,206 @@
+import math
+from contextlib import ExitStack
+
+import concourse.mybir as mybir
+
+F32 = mybir.dt.float32
+I32 = mybir.dt.int32
+U8 = mybir.dt.uint8
+FP4X4 = mybir.dt.float4_e2m1fn_x4
+ALU = mybir.AluOpType
+ACT = mybir.ActivationFunctionType
+
+P = 128
+G = 8
+L = 512
+DK = 1024
+BH = 4
+NT = 4
+N = 512
+TWO_PI = 2.0 * math.pi
+
+FLOPS = 2 * 2048 * 4096 * 2048
+
+
+def tile_retention_pa_kernel(tc, x_words, x_scales, q_words, q_scales, k_words, k_scales, out_q, out_k):
+    nc = tc.nc
+    outs = {"q": out_q.flatten_outer_dims(), "k": out_k.flatten_outer_dims()}
+    outs = {s: (o if o.ndim == 2 else o.rearrange("a b c -> (a b) c")) for s, o in outs.items()}
+
+    with ExitStack() as ctx:
+        ctx.enter_context(tc.manual_schedule())
+        keep = ctx.enter_context(tc.tile_pool(name="keep", bufs=1))
+        tmp = ctx.enter_context(tc.tile_pool(name="tmp", bufs=2))
+        work = ctx.enter_context(tc.tile_pool(name="work", bufs=3))
+        psum = ctx.enter_context(tc.psum_pool(name="psum", bufs=8))
+
+        xc = [keep.tile([P, G, 2 * L], U8, name="xc%d" % b, align_bytes=256) for b in range(BH)]
+        xs = [keep.tile([P, G, L], U8, name="xs%d" % b, align_bytes=256) for b in range(BH)]
+        wc = {s: keep.tile([P, G, 2 * DK], U8, name="wc_" + s, align_bytes=256) for s in "qk"}
+        ws = {s: keep.tile([P, G, DK], U8, name="ws_" + s, align_bytes=256) for s in "qk"}
+        w_words = {"q": q_words, "k": k_words}
+        w_scales = {"q": q_scales, "k": k_scales}
+
+        def zero(engine, tile, g0, g1):
+            engine.memset(tile[:, g0:g1, :].bitcast(I32), 0)
+
+        chunks = [(0, 2), (2, 5), (5, 8)]
+        for g0, g1 in chunks:
+            zero(nc.vector, xs[0], g0, g1)
+            zero(nc.vector, ws["q"], g0, g1)
+        pos = keep.tile([P, NT], F32, name="pos")
+        nc.gpsimd.iota(pos[:], pattern=[[P, NT]], base=0, channel_multiplier=1, allow_small_or_imprecise_dtypes=True)
+        zero(nc.gpsimd, ws["k"], 0, G)
+        for b in range(1, BH):
+            zero(nc.gpsimd, xs[b], 0, G)
+
+        def load(dst, src):
+            nc.sync.dma_start(out=dst.bitcast(I32), in_=src.bitcast(I32))
+
+        def load_x(b, g0, g1):
+            load(xc[b][:, g0:g1, :], x_words[g0:g1, :, 2 * L * b : 2 * L * (b + 1)].rearrange("g p c -> p g c"))
+
+        def load_w(s, g0, g1):
+            load(wc[s][:, g0:g1, :], w_words[s][g0:g1, :, :].rearrange("g p c -> p g c"))
+
+        def load_xs(b, g0, g1):
+            for q in range(4):
+                load(
+                    xs[b][32 * q : 32 * q + 4, g0:g1, :],
+                    x_scales[g0:g1, 4 * q : 4 * q + 4, L * b : L * (b + 1)].rearrange("g r c -> r g c"),
+                )
+
+        def load_ws(s, g0, g1):
+            for q in range(4):
+                load(
+                    ws[s][32 * q : 32 * q + 4, g0:g1, :],
+                    w_scales[s][g0:g1, 4 * q : 4 * q + 4, :].rearrange("g r c -> r g c"),
+                )
+
+        load_x(0, 0, 1)
+        load_w("q", 0, 1)
+        load_xs(0, 0, 2)
+        load_ws("q", 0, 2)
+        load_x(0, 1, 2)
+        load_w("q", 1, 2)
+        load_x(0, 2, 3)
+        load_w("q", 2, 3)
+        load_xs(0, 2, 5)
+        load_ws("q", 2, 5)
+        load_x(0, 3, 5)
+        load_w("q", 3, 5)
+        load_xs(0, 5, 8)
+        load_ws("q", 5, 8)
+        load_x(0, 5, 8)
+        load_w("q", 5, 8)
+        load_ws("k", 0, 8)
+        load_w("k", 0, 4)
+        load_w("k", 4, 8)
+        for b in range(1, BH):
+            load_xs(b, 0, 8)
+            load_x(b, 0, 8)
+
+        freq = keep.tile([P, 2 * L], F32, name="freq")
+        nc.vector.memset(freq[:, 0:1], 1.0)
+        nc.vector.memset(freq[:, 1:2], -1.0)
+        n = 1
+        while n < L:
+            nc.vector.tensor_scalar(
+                out=freq[:, 2 * n : 4 * n], in0=freq[:, 0 : 2 * n], scalar1=10000.0 ** (-n / 511.0), scalar2=None, op0=ALU.mult
+            )
+            n *= 2
+        cos = [keep.tile([P, L], F32, name="cos%d" % j) for j in range(NT)]
+        sin = [keep.tile([P, 2 * L], F32, name="sin%d" % j) for j in range(NT)]
+
+        def turns(j):
+            u = tmp.tile([P, 2 * L], F32, name="u")
+            k = tmp.tile([P, 2 * L], I32, name="k")
+            r = tmp.tile([P, 2 * L], F32, name="r")
+            a = tmp.tile([P, L], F32, name="a")
+            nc.vector.tensor_scalar(out=u[:], in0=freq[:], scalar1=pos[:, j : j + 1], scalar2=1.0 / TWO_PI, op0=ALU.mult, op1=ALU.mult)
+            nc.vector.tensor_copy(out=k[:], in_=u[:])
+            nc.vector.tensor_tensor(out=r[:], in0=u[:], in1=k[:], op=ALU.subtract)
+            nc.scalar.activation(out=a[:], in_=r[:, 0 : 2 * L : 2], func=ACT.Abs)
+            nc.scalar.activation(out=sin[j][:], in_=r[:], func=ACT.Sin, scale=TWO_PI)
+            return a
+
+        def quarter(j, a):
+            v = tmp.tile([P, L], F32, name="v")
+            nc.vector.tensor_scalar(out=v[:], in0=a[:], scalar1=-1.0, scalar2=0.25, op0=ALU.mult, op1=ALU.add)
+            nc.scalar.activation(out=cos[j][:], in_=v[:], func=ACT.Sin, scale=TWO_PI)
+
+        prev = None
+        for j in range(NT):
+            a = turns(j)
+            if prev is not None:
+                quarter(*prev)
+            prev = (j, a)
+        quarter(*prev)
+
+        def mm(acc, b, j, s, g, c0, w):
+            nc.tensor.matmul_mx(
+                out=acc[:, :w],
+                lhsT=xc[b][:, g, 2 * P * j : 2 * P * (j + 1)].bitcast(FP4X4),
+                lhsT_scale=xs[b][:, g, P * j : P * (j + 1)],
+                rhs=wc[s][:, g, 2 * c0 : 2 * (c0 + w)].bitcast(FP4X4),
+                rhs_scale=ws[s][:, g, c0 : c0 + w],
+                start=(g == 0),
+                stop=(g == G - 1),
+            )
+
+        def group(b, j, s, c0, w):
+            acc = psum.tile([P, N], F32, name="acc")
+            for g in range(G):
+                mm(acc, b, j, s, g, c0, w)
+            return acc
+
+        def rotate(acc, j, c0, w, t1, t2):
+            pairs = "p (n two) -> p n two"
+            nc.vector.tensor_tensor(
+                out=t1.rearrange(pairs, two=2),
+                in0=acc[:, :w].rearrange(pairs, two=2),
+                in1=cos[j][:, c0 // 2 : (c0 + w) // 2].unsqueeze(2).to_broadcast([P, w // 2, 2]),
+                op=ALU.mult,
+            )
+            nc.vector.tensor_tensor(out=t2, in0=acc[:, :w], in1=sin[j][:, c0 : c0 + w], op=ALU.mult)
+
+        def finish(s, b, j, c0, w, t1, t2):
+            pairs = "p (n two) -> p n two"
+            o = work.tile([P, DK], F32, name="o")
+            nc.vector.tensor_tensor(
+                out=o[:, :w].rearrange(pairs, two=2),
+                in0=t1.rearrange(pairs, two=2),
+                in1=t2.rearrange(pairs, two=2)[:, :, ::-1],
+                op=ALU.add if s == "q" else ALU.subtract,
+            )
+            row = L * b + P * j
+            nc.sync.dma_start(out=outs[s][row : row + P, c0 : c0 + w], in_=o[:, :w])
+
+        def epilogue(s, b, j, c0, accs):
+            t1 = work.tile([P, DK], F32, name="t1")
+            t2 = work.tile([P, DK], F32, name="t2")
+            at = 0
+            for acc, w in accs:
+                rotate(acc, j, c0 + at, w, t1[:, at : at + w], t2[:, at : at + w])
+                at += w
+            finish(s, b, j, c0, at, t1[:, :at], t2[:, :at])
+
+        first = {}
+        for g in range(G):
+            for j in range(NT):
+                for h in range(2):
+                    if g == 0:
+                        acc = psum.tile([P, N], F32, name="acc")
+                        first[j, h] = acc
+                    mm(first[j, h], 0, j, "q", g, h * N, N)
+        for j in range(NT):
+            epilogue("q", 0, j, 0, [(first[j, 0], N), (first[j, 1], N)])
+
+        for b in range(BH):
+            for j in range(NT):
+                for s in "qk" if b else "k":
+                    if (b, j, s) == (BH - 1, NT - 1, "k"):
+                        for c0, w in ((0, 512), (512, 256), (768, 128), (896, 128)):
+                            epilogue(s, b, j, c0, [(group(b, j, s, c0, w), w)])
+                    else:
+                        epilogue(s, b, j, 0, [(group(b, j, s, h * N, N), N) for h in range(2)])

@@ -6,6 +6,7 @@ import concourse.mybir as mybir
 F32 = mybir.dt.float32
 I32 = mybir.dt.int32
 U8 = mybir.dt.uint8
+BF16 = mybir.dt.bfloat16
 FP4X4 = mybir.dt.float4_e2m1fn_x4
 ALU = mybir.AluOpType
 ACT = mybir.ActivationFunctionType
@@ -44,8 +45,11 @@ def tile_retention_pa_kernel(tc, x_words, x_scales, q_words, q_scales, k_words, 
         def zero(engine, tile, g0, g1):
             engine.memset(tile[:, g0:g1, :].bitcast(I32), 0)
 
-        chunks = [(0, 2), (2, 5), (5, 8)]
-        for g0, g1 in chunks:
+        idle = keep.tile([P, N], BF16, name="idle")
+        zero(nc.vector, xs[0], 0, 2)
+        zero(nc.vector, ws["q"], 0, 2)
+        nc.vector.memset(idle[:], 0.0)
+        for g0, g1 in ((2, 5), (5, 8)):
             zero(nc.vector, xs[0], g0, g1)
             zero(nc.vector, ws["q"], g0, g1)
         pos = keep.tile([P, NT], F32, name="pos")
@@ -60,8 +64,8 @@ def tile_retention_pa_kernel(tc, x_words, x_scales, q_words, q_scales, k_words, 
         def load_x(b, g0, g1):
             load(xc[b][:, g0:g1, :], x_words[g0:g1, :, 2 * L * b : 2 * L * (b + 1)].rearrange("g p c -> p g c"))
 
-        def load_w(s, g0, g1):
-            load(wc[s][:, g0:g1, :], w_words[s][g0:g1, :, :].rearrange("g p c -> p g c"))
+        def load_w(s, g0, g1, b0=0, b1=2 * DK):
+            load(wc[s][:, g0:g1, b0:b1], w_words[s][g0:g1, :, b0:b1].rearrange("g p c -> p g c"))
 
         def load_xs(b, g0, g1):
             for q in range(4):
@@ -78,9 +82,10 @@ def tile_retention_pa_kernel(tc, x_words, x_scales, q_words, q_scales, k_words, 
                 )
 
         load_x(0, 0, 1)
-        load_w("q", 0, 1)
+        load_w("q", 0, 1, 0, DK)
         load_xs(0, 0, 2)
         load_ws("q", 0, 2)
+        load_w("q", 0, 1, DK, 2 * DK)
         load_x(0, 1, 2)
         load_w("q", 1, 2)
         load_x(0, 2, 3)
@@ -185,22 +190,39 @@ def tile_retention_pa_kernel(tc, x_words, x_scales, q_words, q_scales, k_words, 
                 at += w
             finish(s, b, j, c0, at, t1[:, :at], t2[:, :at])
 
+        acc = psum.tile([P, N], F32, name="acc")
+        for i in range(8):
+            nc.tensor.matmul(out=acc[:], lhsT=idle[:, :P], rhs=idle[:], start=True, stop=True)
+
         first = {}
         for g in range(G):
-            for j in range(NT):
-                for h in range(2):
-                    if g == 0:
-                        acc = psum.tile([P, N], F32, name="acc")
-                        first[j, h] = acc
-                    mm(first[j, h], 0, j, "q", g, h * N, N)
+            order = [(j, h) for j in range(NT) for h in range(2)] if g else [(j, h) for h in range(2) for j in range(NT)]
+            for j, h in order:
+                if g == 0:
+                    acc = psum.tile([P, N], F32, name="acc")
+                    first[j, h] = acc
+                mm(first[j, h], 0, j, "q", g, h * N, N)
         for j in range(NT):
             epilogue("q", 0, j, 0, [(first[j, 0], N), (first[j, 1], N)])
 
+        last = []
         for b in range(BH):
             for j in range(NT):
                 for s in "qk" if b else "k":
-                    if (b, j, s) == (BH - 1, NT - 1, "k"):
-                        for c0, w in ((0, 512), (512, 256), (768, 128), (896, 128)):
-                            epilogue(s, b, j, c0, [(group(b, j, s, c0, w), w)])
+                    if (b, j) == (BH - 1, NT - 1):
+                        c0 = 0
+                        for w in (512, 512) if s == "q" else (256, 256, 256, 128, 128):
+                            acc = group(b, j, s, c0, w)
+                            t1 = work.tile([P, DK], F32, name="t1")
+                            t2 = work.tile([P, DK], F32, name="t2")
+                            rotate(acc, j, c0, w, t1[:, :w], t2[:, :w])
+                            if w == N:
+                                finish(s, b, j, c0, w, t1[:, :w], t2[:, :w])
+                            else:
+                                if last:
+                                    finish(*last.pop())
+                                last.append((s, b, j, c0, w, t1[:, :w], t2[:, :w]))
+                            c0 += w
                     else:
                         epilogue(s, b, j, 0, [(group(b, j, s, h * N, N), N) for h in range(2)])
+        finish(*last.pop())

@@ -54,9 +54,6 @@ def tile_retention_pa_kernel(tc, x_words, x_scales, q_words, q_scales, k_words, 
             zero(nc.vector, ws["q"], g0, g1)
         pos = keep.tile([P, NT], F32, name="pos")
         nc.gpsimd.iota(pos[:], pattern=[[P, NT]], base=0, channel_multiplier=1, allow_small_or_imprecise_dtypes=True)
-        zero(nc.gpsimd, ws["k"], 0, G)
-        for b in range(1, BH):
-            zero(nc.gpsimd, xs[b], 0, G)
 
         def load(dst, src):
             nc.sync.dma_start(out=dst.bitcast(I32), in_=src.bitcast(I32))
@@ -68,14 +65,14 @@ def tile_retention_pa_kernel(tc, x_words, x_scales, q_words, q_scales, k_words, 
             load(wc[s][:, g0:g1, b0:b1], w_words[s][g0:g1, :, b0:b1].rearrange("g p c -> p g c"))
 
         def load_xs(b, g0, g1):
-            for q in range(4):
+            for q in (0, 2, 1, 3):
                 load(
                     xs[b][32 * q : 32 * q + 4, g0:g1, :],
                     x_scales[g0:g1, 4 * q : 4 * q + 4, L * b : L * (b + 1)].rearrange("g r c -> r g c"),
                 )
 
         def load_ws(s, g0, g1):
-            for q in range(4):
+            for q in (0, 2, 1, 3):
                 load(
                     ws[s][32 * q : 32 * q + 4, g0:g1, :],
                     w_scales[s][g0:g1, 4 * q : 4 * q + 4, :].rearrange("g r c -> r g c"),
@@ -98,22 +95,21 @@ def tile_retention_pa_kernel(tc, x_words, x_scales, q_words, q_scales, k_words, 
         load_ws("q", 5, 8)
         load_x(0, 5, 8)
         load_w("q", 5, 8)
-        load_ws("k", 0, 8)
-        load_w("k", 0, 4)
-        load_w("k", 4, 8)
-        for b in range(1, BH):
-            load_xs(b, 0, 8)
-            load_x(b, 0, 8)
 
         freq = keep.tile([P, 2 * L], F32, name="freq")
         nc.vector.memset(freq[:, 0:1], 1.0)
         nc.vector.memset(freq[:, 1:2], -1.0)
-        n = 1
+        n, g = 1, 0
         while n < L:
             nc.vector.tensor_scalar(
                 out=freq[:, 2 * n : 4 * n], in0=freq[:, 0 : 2 * n], scalar1=10000.0 ** (-n / 511.0), scalar2=None, op0=ALU.mult
             )
-            n *= 2
+            if g < G:
+                zero(nc.vector, ws["k"], g, g + 1)
+            n, g = 2 * n, g + 1
+        load_ws("k", 0, 8)
+        load_w("k", 0, 4)
+        load_w("k", 4, 8)
         cos = [keep.tile([P, L], F32, name="cos%d" % j) for j in range(NT)]
         sin = [keep.tile([P, 2 * L], F32, name="sin%d" % j) for j in range(NT)]
 
@@ -139,6 +135,10 @@ def tile_retention_pa_kernel(tc, x_words, x_scales, q_words, q_scales, k_words, 
             a = turns(j)
             if prev is not None:
                 quarter(*prev)
+            if j == 1:
+                zero(nc.vector, xs[1], 0, G)
+                load_xs(1, 0, 8)
+                load_x(1, 0, 8)
             prev = (j, a)
         quarter(*prev)
 
@@ -169,10 +169,10 @@ def tile_retention_pa_kernel(tc, x_words, x_scales, q_words, q_scales, k_words, 
             )
             nc.vector.tensor_tensor(out=t2, in0=acc[:, :w], in1=sin[j][:, c0 : c0 + w], op=ALU.mult)
 
-        def finish(s, b, j, c0, w, t1, t2):
+        def finish(s, b, j, c0, w, t1, t2, engine=nc.vector):
             pairs = "p (n two) -> p n two"
             o = work.tile([P, DK], F32, name="o")
-            nc.vector.tensor_tensor(
+            engine.tensor_tensor(
                 out=o[:, :w].rearrange(pairs, two=2),
                 in0=t1.rearrange(pairs, two=2),
                 in1=t2.rearrange(pairs, two=2)[:, :, ::-1],
@@ -208,6 +208,10 @@ def tile_retention_pa_kernel(tc, x_words, x_scales, q_words, q_scales, k_words, 
         last = []
         for b in range(BH):
             for j in range(NT):
+                if j == 2 and b + 2 < BH:
+                    zero(nc.vector, xs[b + 2], 0, G)
+                    load_xs(b + 2, 0, 8)
+                    load_x(b + 2, 0, 8)
                 for s in "qk" if b else "k":
                     if (b, j) == (BH - 1, NT - 1):
                         c0 = 0
@@ -216,8 +220,8 @@ def tile_retention_pa_kernel(tc, x_words, x_scales, q_words, q_scales, k_words, 
                             t1 = work.tile([P, DK], F32, name="t1")
                             t2 = work.tile([P, DK], F32, name="t2")
                             rotate(acc, j, c0, w, t1[:, :w], t2[:, :w])
-                            if w == N:
-                                finish(s, b, j, c0, w, t1[:, :w], t2[:, :w])
+                            if s == "q" or c0 < 512:
+                                finish(s, b, j, c0, w, t1[:, :w], t2[:, :w], nc.gpsimd)
                             else:
                                 if last:
                                     finish(*last.pop())

@@ -32,7 +32,8 @@ def tile_retention_pa_kernel(tc, x_words, x_scales, q_words, q_scales, k_words, 
         ctx.enter_context(tc.manual_schedule())
         keep = ctx.enter_context(tc.tile_pool(name="keep", bufs=1))
         tmp = ctx.enter_context(tc.tile_pool(name="tmp", bufs=2))
-        work = ctx.enter_context(tc.tile_pool(name="work", bufs=3))
+        work = ctx.enter_context(tc.tile_pool(name="work", bufs=4))
+        store = ctx.enter_context(tc.tile_pool(name="store", bufs=6))
         psum = ctx.enter_context(tc.psum_pool(name="psum", bufs=8))
 
         xc = [keep.tile([P, G, 2 * L], U8, name="xc%d" % b, align_bytes=256) for b in range(BH)]
@@ -135,10 +136,6 @@ def tile_retention_pa_kernel(tc, x_words, x_scales, q_words, q_scales, k_words, 
             a = turns(j)
             if prev is not None:
                 quarter(*prev)
-            if j == 1:
-                zero(nc.vector, xs[1], 0, G)
-                load_xs(1, 0, 8)
-                load_x(1, 0, 8)
             prev = (j, a)
         quarter(*prev)
 
@@ -171,7 +168,7 @@ def tile_retention_pa_kernel(tc, x_words, x_scales, q_words, q_scales, k_words, 
 
         def finish(s, b, j, c0, w, t1, t2, engine=nc.vector):
             pairs = "p (n two) -> p n two"
-            o = work.tile([P, DK], F32, name="o")
+            o = store.tile([P, DK], F32, name="o")
             engine.tensor_tensor(
                 out=o[:, :w].rearrange(pairs, two=2),
                 in0=t1.rearrange(pairs, two=2),
@@ -191,7 +188,7 @@ def tile_retention_pa_kernel(tc, x_words, x_scales, q_words, q_scales, k_words, 
             finish(s, b, j, c0, at, t1[:, :at], t2[:, :at])
 
         acc = psum.tile([P, N], F32, name="acc")
-        for i in range(8):
+        for i in range(6):
             nc.tensor.matmul(out=acc[:], lhsT=idle[:, :P], rhs=idle[:], start=True, stop=True)
 
         first = {}
@@ -204,6 +201,10 @@ def tile_retention_pa_kernel(tc, x_words, x_scales, q_words, q_scales, k_words, 
                 mm(first[j, h], 0, j, "q", g, h * N, N)
         for j in range(NT):
             epilogue("q", 0, j, 0, [(first[j, 0], N), (first[j, 1], N)])
+            if j == 0:
+                zero(nc.vector, xs[1], 0, G)
+                load_xs(1, 0, 8)
+                load_x(1, 0, 8)
 
         last = []
         for b in range(BH):

import math
from contextlib import ExitStack

import concourse.mybir as mybir

F32 = mybir.dt.float32
I32 = mybir.dt.int32
U8 = mybir.dt.uint8
BF16 = mybir.dt.bfloat16
FP4X4 = mybir.dt.float4_e2m1fn_x4
ALU = mybir.AluOpType
ACT = mybir.ActivationFunctionType

P = 128
G = 8
L = 512
DK = 1024
BH = 4
NT = 4
N = 512
TWO_PI = 2.0 * math.pi

FLOPS = 2 * 2048 * 4096 * 2048


def tile_retention_pa_kernel(tc, x_words, x_scales, q_words, q_scales, k_words, k_scales, out_q, out_k):
    nc = tc.nc
    outs = {"q": out_q.flatten_outer_dims(), "k": out_k.flatten_outer_dims()}
    outs = {s: (o if o.ndim == 2 else o.rearrange("a b c -> (a b) c")) for s, o in outs.items()}

    with ExitStack() as ctx:
        ctx.enter_context(tc.manual_schedule())
        keep = ctx.enter_context(tc.tile_pool(name="keep", bufs=1))
        tmp = ctx.enter_context(tc.tile_pool(name="tmp", bufs=2))
        work = ctx.enter_context(tc.tile_pool(name="work", bufs=4))
        store = ctx.enter_context(tc.tile_pool(name="store", bufs=6))
        psum = ctx.enter_context(tc.psum_pool(name="psum", bufs=8))

        xc = [keep.tile([P, G, 2 * L], U8, name="xc%d" % b, align_bytes=256) for b in range(BH)]
        xs = [keep.tile([P, G, L], U8, name="xs%d" % b, align_bytes=256) for b in range(BH)]
        wc = {s: keep.tile([P, G, 2 * DK], U8, name="wc_" + s, align_bytes=256) for s in "qk"}
        ws = {s: keep.tile([P, G, DK], U8, name="ws_" + s, align_bytes=256) for s in "qk"}
        w_words = {"q": q_words, "k": k_words}
        w_scales = {"q": q_scales, "k": k_scales}

        def zero(engine, tile, g0, g1):
            engine.memset(tile[:, g0:g1, :].bitcast(I32), 0)

        idle = keep.tile([P, N], BF16, name="idle")
        zero(nc.vector, xs[0], 0, 2)
        zero(nc.vector, ws["q"], 0, 2)
        nc.vector.memset(idle[:], 0.0)
        for g0, g1 in ((2, 5), (5, 8)):
            zero(nc.vector, xs[0], g0, g1)
            zero(nc.vector, ws["q"], g0, g1)
        pos = keep.tile([P, NT], F32, name="pos")
        nc.gpsimd.iota(pos[:], pattern=[[P, NT]], base=0, channel_multiplier=1, allow_small_or_imprecise_dtypes=True)

        def load(dst, src):
            nc.sync.dma_start(out=dst.bitcast(I32), in_=src.bitcast(I32))

        def load_x(b, g0, g1):
            load(xc[b][:, g0:g1, :], x_words[g0:g1, :, 2 * L * b : 2 * L * (b + 1)].rearrange("g p c -> p g c"))

        def load_w(s, g0, g1, b0=0, b1=2 * DK):
            load(wc[s][:, g0:g1, b0:b1], w_words[s][g0:g1, :, b0:b1].rearrange("g p c -> p g c"))

        def load_xs(b, g0, g1):
            for q in (0, 2, 1, 3):
                load(
                    xs[b][32 * q : 32 * q + 4, g0:g1, :],
                    x_scales[g0:g1, 4 * q : 4 * q + 4, L * b : L * (b + 1)].rearrange("g r c -> r g c"),
                )

        def load_ws(s, g0, g1):
            for q in (0, 2, 1, 3):
                load(
                    ws[s][32 * q : 32 * q + 4, g0:g1, :],
                    w_scales[s][g0:g1, 4 * q : 4 * q + 4, :].rearrange("g r c -> r g c"),
                )

        load_x(0, 0, 1)
        load_w("q", 0, 1, 0, DK)
        load_xs(0, 0, 2)
        load_ws("q", 0, 2)
        load_w("q", 0, 1, DK, 2 * DK)
        load_x(0, 1, 2)
        load_w("q", 1, 2)
        load_x(0, 2, 3)
        load_w("q", 2, 3)
        load_xs(0, 2, 5)
        load_ws("q", 2, 5)
        load_x(0, 3, 5)
        load_w("q", 3, 5)
        load_xs(0, 5, 8)
        load_ws("q", 5, 8)
        load_x(0, 5, 8)
        load_w("q", 5, 8)

        freq = keep.tile([P, 2 * L], F32, name="freq")
        nc.vector.memset(freq[:, 0:1], 1.0)
        nc.vector.memset(freq[:, 1:2], -1.0)
        n, g = 1, 0
        while n < L:
            nc.vector.tensor_scalar(
                out=freq[:, 2 * n : 4 * n], in0=freq[:, 0 : 2 * n], scalar1=10000.0 ** (-n / 511.0), scalar2=None, op0=ALU.mult
            )
            if g < G:
                zero(nc.vector, ws["k"], g, g + 1)
            n, g = 2 * n, g + 1
        load_ws("k", 0, 8)
        load_w("k", 0, 4)
        load_w("k", 4, 8)
        cos = [keep.tile([P, L], F32, name="cos%d" % j) for j in range(NT)]
        sin = [keep.tile([P, 2 * L], F32, name="sin%d" % j) for j in range(NT)]

        def turns(j):
            u = tmp.tile([P, 2 * L], F32, name="u")
            k = tmp.tile([P, 2 * L], I32, name="k")
            r = tmp.tile([P, 2 * L], F32, name="r")
            a = tmp.tile([P, L], F32, name="a")
            nc.vector.tensor_scalar(out=u[:], in0=freq[:], scalar1=pos[:, j : j + 1], scalar2=1.0 / TWO_PI, op0=ALU.mult, op1=ALU.mult)
            nc.vector.tensor_copy(out=k[:], in_=u[:])
            nc.vector.tensor_tensor(out=r[:], in0=u[:], in1=k[:], op=ALU.subtract)
            nc.scalar.activation(out=a[:], in_=r[:, 0 : 2 * L : 2], func=ACT.Abs)
            nc.scalar.activation(out=sin[j][:], in_=r[:], func=ACT.Sin, scale=TWO_PI)
            return a

        def quarter(j, a):
            v = tmp.tile([P, L], F32, name="v")
            nc.vector.tensor_scalar(out=v[:], in0=a[:], scalar1=-1.0, scalar2=0.25, op0=ALU.mult, op1=ALU.add)
            nc.scalar.activation(out=cos[j][:], in_=v[:], func=ACT.Sin, scale=TWO_PI)

        prev = None
        for j in range(NT):
            a = turns(j)
            if prev is not None:
                quarter(*prev)
            prev = (j, a)
        quarter(*prev)

        def mm(acc, b, j, s, g, c0, w):
            nc.tensor.matmul_mx(
                out=acc[:, :w],
                lhsT=xc[b][:, g, 2 * P * j : 2 * P * (j + 1)].bitcast(FP4X4),
                lhsT_scale=xs[b][:, g, P * j : P * (j + 1)],
                rhs=wc[s][:, g, 2 * c0 : 2 * (c0 + w)].bitcast(FP4X4),
                rhs_scale=ws[s][:, g, c0 : c0 + w],
                start=(g == 0),
                stop=(g == G - 1),
            )

        def group(b, j, s, c0, w):
            acc = psum.tile([P, N], F32, name="acc")
            for g in range(G):
                mm(acc, b, j, s, g, c0, w)
            return acc

        def rotate(acc, j, c0, w, t1, t2):
            pairs = "p (n two) -> p n two"
            nc.vector.tensor_tensor(
                out=t1.rearrange(pairs, two=2),
                in0=acc[:, :w].rearrange(pairs, two=2),
                in1=cos[j][:, c0 // 2 : (c0 + w) // 2].unsqueeze(2).to_broadcast([P, w // 2, 2]),
                op=ALU.mult,
            )
            nc.vector.tensor_tensor(out=t2, in0=acc[:, :w], in1=sin[j][:, c0 : c0 + w], op=ALU.mult)

        def finish(s, b, j, c0, w, t1, t2, engine=nc.vector):
            pairs = "p (n two) -> p n two"
            o = store.tile([P, DK], F32, name="o")
            engine.tensor_tensor(
                out=o[:, :w].rearrange(pairs, two=2),
                in0=t1.rearrange(pairs, two=2),
                in1=t2.rearrange(pairs, two=2)[:, :, ::-1],
                op=ALU.add if s == "q" else ALU.subtract,
            )
            row = L * b + P * j
            nc.sync.dma_start(out=outs[s][row : row + P, c0 : c0 + w], in_=o[:, :w])

        def epilogue(s, b, j, c0, accs):
            t1 = work.tile([P, DK], F32, name="t1")
            t2 = work.tile([P, DK], F32, name="t2")
            at = 0
            for acc, w in accs:
                rotate(acc, j, c0 + at, w, t1[:, at : at + w], t2[:, at : at + w])
                at += w
            finish(s, b, j, c0, at, t1[:, :at], t2[:, :at])

        acc = psum.tile([P, N], F32, name="acc")
        for i in range(6):
            nc.tensor.matmul(out=acc[:], lhsT=idle[:, :P], rhs=idle[:], start=True, stop=True)

        first = {}
        for g in range(G):
            order = [(j, h) for j in range(NT) for h in range(2)] if g else [(j, h) for h in range(2) for j in range(NT)]
            for j, h in order:
                if g == 0:
                    acc = psum.tile([P, N], F32, name="acc")
                    first[j, h] = acc
                mm(first[j, h], 0, j, "q", g, h * N, N)
        for j in range(NT):
            epilogue("q", 0, j, 0, [(first[j, 0], N), (first[j, 1], N)])
            if j == 0:
                zero(nc.vector, xs[1], 0, G)
                load_xs(1, 0, 8)
                load_x(1, 0, 8)

        last = []
        for b in range(BH):
            for j in range(NT):
                if j == 2 and b + 2 < BH:
                    zero(nc.vector, xs[b + 2], 0, G)
                    load_xs(b + 2, 0, 8)
                    load_x(b + 2, 0, 8)
                for s in "qk" if b else "k":
                    if (b, j) == (BH - 1, NT - 1):
                        c0 = 0
                        for w in (512, 512) if s == "q" else (256, 256, 256, 128, 128):
                            acc = group(b, j, s, c0, w)
                            t1 = work.tile([P, DK], F32, name="t1")
                            t2 = work.tile([P, DK], F32, name="t2")
                            rotate(acc, j, c0, w, t1[:, :w], t2[:, :w])
                            if s == "q" or c0 < 512:
                                finish(s, b, j, c0, w, t1[:, :w], t2[:, :w], nc.gpsimd)
                            else:
                                if last:
                                    finish(*last.pop())
                                last.append((s, b, j, c0, w, t1[:, :w], t2[:, :w]))
                            c0 += w
                    else:
                        epilogue(s, b, j, 0, [(group(b, j, s, h * N, N), N) for h in range(2)])
        finish(*last.pop())
